import numpy as np
import ml_dtypes


def mxq(x, axis, fmt="e4m3"):
    dtype, down = {"e4m3": (ml_dtypes.float8_e4m3fn, 7), "e5m2": (ml_dtypes.float8_e5m2, 14)}[fmt]
    v = np.moveaxis(np.asarray(x, np.float32).astype(ml_dtypes.bfloat16).astype(np.float64), axis, -1)
    blocks = v.reshape(v.shape[:-1] + (-1, 32))
    amax = np.abs(blocks).max(-1, keepdims=True)
    byte = np.maximum(np.where(amax > 0, np.frexp(amax)[1] - 1 + 127, 0) - down, 1)
    scale = np.exp2(byte - 127.0)
    codes = (blocks / scale).astype(np.float32).astype(dtype).astype(np.float64)
    return np.moveaxis((codes * scale).reshape(v.shape), -1, axis)


WIDE = False


def mx_kscale(k):
    if not WIDE:
        return np.ones(k)
    levels = np.array([10, -10, 5, -5, 0])
    if k % 512:
        return np.exp2(np.random.permutation(np.resize(levels, k // 32))).repeat(32)
    a = np.empty((k // 512, 16))
    for p in range(k // 512):
        a[p, :8] = np.random.permutation(np.resize(levels, 8))
        for g in range(8):
            far = levels[np.abs(levels - a[p, g]) >= 10]
            a[p, g + 8] = far[np.random.randint(len(far))]
    return np.exp2(a.ravel()).repeat(32)


BF16 = ml_dtypes.bfloat16


def bf(x):
    return np.asarray(x, np.float32).astype(BF16)


def f64(x):
    return np.asarray(x).astype(np.float64)


B, F, HH, WW, DI, DM, DH, T, SF, LOC, SINK = 1, 4, 16, 32, 1024, 1024, 128, 64, 2, 2, 1
L = F * HH * WW
NH = DM // DH
C = DH // 2
C1 = C // 3
C0 = C - 2 * C1
EPS = 1e-6


def rms_norm(t, g):
    return t * (1.0 / np.sqrt(np.mean(t * t, axis=-1, keepdims=True) + EPS)) * g


def rope_apply(t, angles):
    af = angles[SF:SF + F, :C0]
    ah = angles[:HH, C0:C0 + C1]
    aw = angles[:WW, C0 + C1:]
    ang = np.concatenate([
        np.broadcast_to(af[:, None, None, :], (F, HH, WW, C0)),
        np.broadcast_to(ah[None, :, None, :], (F, HH, WW, C1)),
        np.broadcast_to(aw[None, None, :, :], (F, HH, WW, C1)),
    ], axis=-1).reshape(1, L, 1, C)
    cos, sin = np.cos(ang), np.sin(ang)
    tr = t.reshape(B, L, NH, C, -1)
    re, im = tr[..., 0], tr[..., 1]
    res = np.stack([re * cos - im * sin, re * sin + im * cos], axis=-1)
    return res.reshape(B, L, NH, DH)


def draw0():
    s = mx_kscale(DI)
    return {
        'x': bf(np.random.standard_normal((B, L, DI)) * s),
        'freqs': bf(np.random.uniform(-3.0, 3.0, (T, C))),
        'Wq': bf(np.random.standard_normal((DM, DI)) / np.sqrt(DI) / s[None, :]),
        'bq': bf(np.random.standard_normal(DM) * 0.3),
        'Wk': bf(np.random.standard_normal((DM, DI)) / np.sqrt(DI) / s[None, :]),
        'bk': bf(np.random.standard_normal(DM) * 0.3),
        'gq': bf(1.5 + 0.2 * np.random.standard_normal(DM)),
        'gk': bf(1.5 + 0.2 * np.random.standard_normal(DM)),
    }


def core(x, freqs, Wq, bq, Wk, bk, gq, gk):
    xq = mxq(f64(x), 2, 'e4m3')
    q = rms_norm((xq @ mxq(f64(Wq), 1, 'e4m3').T) + f64(bq), f64(gq)).reshape(B, L, NH, DH)
    k = rms_norm((xq @ mxq(f64(Wk), 1, 'e4m3').T) + f64(bk), f64(gk)).reshape(B, L, NH, DH)
    ang = f64(freqs)
    return rope_apply(q, ang), rope_apply(k, ang)


def e4m3fn_bytes(y):
    return np.clip(np.asarray(y, np.float64), -448.0, 448.0).astype(np.float32).astype(ml_dtypes.float8_e4m3fn).view(np.uint8)


def e4m3fn_values(b):
    return np.asarray(b, np.uint8).view(ml_dtypes.float8_e4m3fn).astype(np.float64)


def setup_inputs():
    d = draw0()
    x0 = np.asarray(d['x']).astype(np.float64)
    s = (np.max(np.abs(x0), axis=(0, 1), keepdims=True) / 448.0).astype(np.float32)
    out = {}
    for k, v in d.items():
        if k == 'x':
            out['x_bytes'] = e4m3fn_bytes(x0 / s.astype(np.float64))
            out['x_scale'] = s
        else:
            out[k] = v
    return out


def reference(x_bytes, x_scale, freqs, Wq, bq, Wk, bk, gq, gk):
    return core(e4m3fn_values(x_bytes) * x_scale.astype(np.float64), freqs, Wq, bq, Wk, bk, gq, gk)

@@ -1,0 +1,291 @@
+from contextlib import ExitStack
+import math
+
+import concourse.mybir as mybir
+from concourse.masks import make_identity
+
+F32 = mybir.dt.float32
+BF16 = mybir.dt.bfloat16
+U32 = mybir.dt.uint32
+U8 = mybir.dt.uint8
+FP8 = mybir.dt.float8_e4m3fn
+FP8X4 = mybir.dt.float8_e4m3fn_x4
+ACT = mybir.ActivationFunctionType
+ALU = mybir.AluOpType
+
+P = 128
+L = 2048
+K = 1024
+DM = 1024
+NH = 8
+FRAME = 512
+NFRAME = L // FRAME
+FIRST_FRAME_ROW = 2
+EPS = 1e-6
+NF, NR, NCOL = 22, 21, 21
+NANG = 4 * NF + 4 * NR + NCOL
+ROOT_DM = 32.0
+BANK = 512
+PAIR = 2 * P
+
+FLOPS = 2 * L * K * 2 * DM
+
+
+def tile_causalwanselfattention_pa_kernel(
+    tc, x_bytes, x_scale, freqs, Wq, bq, Wk, bk, gq, gk, out_0, out_1
+):
+    nc = tc.nc
+    xb_dram = x_bytes.rearrange("b l k -> (b l) k")
+    outs = (
+        out_0.rearrange("b l h d -> (b l) (h d)"),
+        out_1.rearrange("b l h d -> (b l) (h d)"),
+    )
+    w_dram = (Wq, Wk)
+
+    with ExitStack() as ctx:
+        const = ctx.enter_context(tc.tile_pool(name="const", bufs=1))
+        xbp = ctx.enter_context(tc.tile_pool(name="xbp", bufs=4))
+        xwp = ctx.enter_context(tc.tile_pool(name="xwp", bufs=3))
+        xgp = ctx.enter_context(tc.tile_pool(name="xgp", bufs=2))
+        wbp = ctx.enter_context(tc.tile_pool(name="wbp", bufs=4))
+        wgp = ctx.enter_context(tc.tile_pool(name="wgp", bufs=3))
+        tpose = ctx.enter_context(tc.tile_pool(name="tpose", bufs=2))
+        mmp = ctx.enter_context(tc.tile_pool(name="mmp", bufs=3))
+        outp = ctx.enter_context(tc.tile_pool(name="outp", bufs=3))
+        small = ctx.enter_context(tc.tile_pool(name="small", bufs=4))
+        psum = ctx.enter_context(tc.psum_pool(name="psum", bufs=8))
+
+        ident = const.tile([P, P], F32, name="ident")
+        make_identity(nc, ident[:])
+        gbrow = const.tile([P, P], BF16, name="gbrow")
+        nc.vector.memset(gbrow[:], 0.0)
+        warm = const.tile([P, 2], F32, name="warm")
+        nc.vector.memset(warm[:], 0.0)
+        nc.scalar.activation(out=warm[:, 1:2], in_=warm[:, 0:1], func=ACT.Sin)
+        xs_bc = const.tile([P, K], F32, name="xs_bc")
+        fcol = const.tile([P, 64], BF16, name="fcol")
+        fr16 = const.tile([P, 16, 64], BF16, name="fr16")
+
+        def load_small():
+            for i, vec in enumerate((gq, gk, bq, bk)):
+                nc.sync.dma_start(out=gbrow[8 * i : 8 * i + 8, :], in_=vec.rearrange("(j p) -> j p", p=P))
+            for q in range(4):
+                nc.sync.dma_start(out=fcol[32 * q : 32 * q + 32, :], in_=freqs[0:32, :])
+            nc.sync.dma_start(
+                out=fr16[:].rearrange("p r c -> p (r c)"),
+                in_=freqs[0:16, :].rearrange("r c -> (r c)").partition_broadcast(P),
+            )
+
+        xb = {}
+        wb = {}
+
+        def load_x(c):
+            t = xbp.tile([P, 4, K], U8, name="xb")
+            nc.sync.dma_start(out=t[:], in_=xb_dram[c * FRAME : (c + 1) * FRAME, :].rearrange("(a p) k -> p a k", p=P))
+            xb[c] = t
+
+        def load_w(hf, pair):
+            t = wbp.tile([P, 2, K], BF16, name="wb")
+            nc.sync.dma_start(
+                out=t[:], in_=w_dram[hf][pair * PAIR : (pair + 1) * PAIR, :].rearrange("(a p) k -> p a k", p=P)
+            )
+            wb[(hf, pair)] = t
+
+        load_w(0, 0)
+        nc.sync.dma_start(out=xs_bc[:], in_=x_scale.rearrange("a b k -> (a b k)").partition_broadcast(P))
+        load_x(0)
+        load_w(0, 1)
+        load_small()
+        load_w(0, 2)
+        load_w(0, 3)
+        load_x(1)
+        load_x(2)
+        load_x(3)
+
+        ident_bf = const.tile([P, P], BF16, name="ident_bf")
+        make_identity(nc, ident_bf[:])
+
+        gbT = const.tile([P, 32], F32, name="gbT")
+        gbp = const.tile([P, 16], F32, name="gbp")
+        b32 = const.tile([P, 16], F32, name="b32")
+        ang = const.tile([P, NANG], F32, name="ang")
+        trig = const.tile([P, 2, NANG, 2], F32, name="trig")
+        absang = const.tile([P, NANG], F32, name="absang")
+        rot = const.tile([P, 16, 2, P], F32, name="rot")
+
+        def setup_gain_bias():
+            gb_ps = psum.tile([P, P], BF16, name="gb_ps", tag="bank")
+            nc.tensor.transpose(gb_ps[:], gbrow[:], ident_bf[:])
+            nc.vector.tensor_copy(out=gbT[:], in_=gb_ps[:, 0:32])
+            nc.vector.tensor_tensor(out=gbp[:], in0=gbT[:, 0:16], in1=gbT[:, 16:32], op=ALU.mult)
+            nc.vector.tensor_scalar(out=b32[:], in0=gbT[:, 16:32], scalar1=1.0 / ROOT_DM, scalar2=None, op0=ALU.mult)
+
+        def setup_rot():
+            rows0 = 4 * NF
+            cols0 = 4 * NF + 4 * NR
+            nc.vector.tensor_copy(
+                out=ang[:, 0:rows0].rearrange("p (f j) -> p f j", f=4),
+                in_=fr16[:, FIRST_FRAME_ROW : FIRST_FRAME_ROW + 4, 0:NF],
+            )
+            for q in range(4):
+                quad = slice(32 * q, 32 * q + 32)
+                nc.vector.tensor_copy(
+                    out=ang[quad, rows0:cols0].rearrange("p (f j) -> p f j", f=4),
+                    in_=fr16[quad, q:16:4, NF : NF + NR],
+                )
+            nc.vector.tensor_copy(out=ang[:, cols0:NANG], in_=fcol[:, NF + NR : 64])
+
+            nc.scalar.activation(out=trig[:, 1, :, 0], in_=ang[:], func=ACT.Sin, scale=-1.0)
+            nc.scalar.activation(out=trig[:, 1, :, 1], in_=ang[:], func=ACT.Sin)
+            nc.scalar.activation(out=absang[:], in_=ang[:], func=ACT.Abs)
+            nc.scalar.activation(
+                out=trig[:, 0, :, :],
+                in_=absang[:].unsqueeze(2).to_broadcast([P, NANG, 2]),
+                func=ACT.Sin,
+                scale=-1.0,
+                bias=math.pi / 2.0,
+            )
+            nc.scalar.activation(out=warm[:, 1:2], in_=trig[:, 0, 0:1, 0], func=ACT.Abs_reciprocal_sqrt, bias=2.0)
+
+            def spread(dst, a0, n, reps):
+                src = trig[:, :, a0 : a0 + n, :].rearrange("p t j e -> p t (j e)")
+                nc.gpsimd.tensor_scalar(
+                    out=dst,
+                    in0=src.unsqueeze(1).to_broadcast([P, reps, 2, 2 * n]),
+                    scalar1=1.0,
+                    scalar2=0.0,
+                    op0=ALU.mult,
+                    op1=ALU.add,
+                )
+
+            row_ch = slice(2 * NF, 2 * (NF + NR))
+            spread(rot[:, 0:4, :, 0 : 2 * NF], 0, NF, 4)
+            spread(rot[:, 0:16:4, :, row_ch], rows0, NR, 4)
+            spread(rot[:, :, :, 2 * (NF + NR) : P], cols0, NCOL, 16)
+            for f in range(1, 4):
+                spread(rot[:, f:16:4, :, row_ch], rows0 + f * NR, NR, 4)
+            for f in range(1, 4):
+                spread(rot[:, 4 * f : 4 * f + 4, :, 0 : 2 * NF], f * NF, NF, 4)
+
+        wq = const.tile([P, 2, 4, 2, PAIR], U32, name="wq", align_bytes=64)
+        wsc = const.tile([P, 2, 4, 2, PAIR], U8, name="wsc", align_bytes=64)
+        xq = const.tile([P, NFRAME, 2, FRAME], U32, name="xq", align_bytes=64)
+        xsc = const.tile([P, NFRAME, 2, FRAME], U8, name="xsc", align_bytes=64)
+
+        def k_to_partitions(words, dst):
+            tp = psum.tile([P, BANK], F32, name="tp", tag="bank")
+            for g in range(2):
+                for u in range(2):
+                    i = 2 * g + u
+                    nc.tensor.transpose(tp[:, i * P : (i + 1) * P], words[:, 256 * g + u : 256 * (g + 1) : 2], ident[:])
+            nc.scalar.copy(out=dst, in_=tp[:].rearrange("p (g u r) -> p g r u", g=2, u=2))
+
+        def quantise(grouped, codes, scales):
+            nc.vector.quantize_mx(
+                out=codes.rearrange("p g r -> p (g r)").bitcast(FP8X4),
+                scales=scales.rearrange("p g r -> p (g r)"),
+                in_=grouped.rearrange("p g r u -> p (g r u)").bitcast(BF16),
+            )
+
+        def prep_w(hf, pair):
+            wg = wgp.tile([P, 2, PAIR, 2], F32, name="wg", align_bytes=64)
+            for hh in range(2):
+                k_to_partitions(wb[(hf, pair)][:, hh, :].bitcast(F32), wg[:, :, hh * P : (hh + 1) * P, :])
+            quantise(wg[:], wq[:, hf, pair, :, :], wsc[:, hf, pair, :, :])
+
+        xg = {}
+
+        def prep_x(c, a):
+            if a == 0:
+                xg[c] = xgp.tile([P, 2, FRAME, 2], F32, name="xg", align_bytes=64)
+            xw = xwp.tile([P, K], BF16, name="xw")
+            nc.vector.tensor_tensor(out=xw[:], in0=xb[c][:, a, :].bitcast(FP8), in1=xs_bc[:], op=ALU.mult)
+            k_to_partitions(xw[:].bitcast(F32), xg[c][:, :, a * P : (a + 1) * P, :])
+            if a == 3:
+                quantise(xg[c][:], xq[:, c, :, :], xsc[:, c, :, :])
+
+        def project(c, hf, t0, n, j, vT, sqT):
+            acc = psum.tile([P, n], F32, name="acc", tag="bank")
+            ch = slice((j % 2) * P, (j % 2 + 1) * P)
+            tok = slice(t0, t0 + n)
+            for g in range(2):
+                nc.tensor.matmul_mx(
+                    out=acc[:],
+                    lhsT=wq[:, hf, j // 2, g, ch].bitcast(FP8X4),
+                    lhsT_scale=wsc[:, hf, j // 2, g, ch],
+                    rhs=xq[:, c, g, tok].bitcast(FP8X4),
+                    rhs_scale=xsc[:, c, g, tok],
+                    start=(g == 0),
+                    stop=(g == 1),
+                )
+            col = slice(8 * hf + j, 8 * hf + j + 1)
+            nc.scalar.activation(out=vT[:, j, :], in_=acc[:], func=ACT.Identity, scale=gbT[:, col], bias=gbp[:, col])
+            nc.scalar.activation(out=sqT[:, j, :], in_=acc[:], func=ACT.Square, scale=1.0 / ROOT_DM, bias=b32[:, col])
+
+        def finish_unit(c, hf, t0, a, vT, sqT, sqacc):
+            t = 4 * c + t0 // P + a
+            tok = slice(a * P, (a + 1) * P)
+            for j in range(NH):
+                nc.tensor.matmul(
+                    out=sqacc[:, tok], lhsT=sqT[:, j, tok], rhs=ident[:], is_transpose=True, start=(j == 0), stop=(j == NH - 1)
+                )
+            banks = []
+            for b in range(2):
+                vb = psum.tile([P, BANK], F32, name="vb", tag="bank")
+                for jj in range(4):
+                    nc.tensor.transpose(vb[:, jj * P : (jj + 1) * P], vT[:, 4 * b + jj, tok], ident[:])
+                banks.append(vb)
+            junk = small.tile([P, P], BF16, name="junk")
+            ms = small.tile([P, 1], F32, name="ms")
+            nc.scalar.activation(out=junk[:], in_=sqacc[:, tok], func=ACT.Copy, accum_out=ms[:])
+            rstd = small.tile([P, 1], F32, name="rstd")
+            nc.scalar.activation(out=rstd[:], in_=ms[:], func=ACT.Abs_reciprocal_sqrt, bias=EPS)
+            prod = mmp.tile([P, 2, DM], F32, name="prod")
+            for b in range(2):
+                for tbl in range(2):
+                    pairs = banks[b][:].rearrange("p (h j e) -> p h j e", h=4, e=2)
+                    nc.vector.scalar_tensor_tensor(
+                        out=prod[:, tbl, b * BANK : (b + 1) * BANK].rearrange("p (h j e) -> p h j e", h=4, e=2),
+                        in0=pairs if tbl == 0 else pairs[:, :, :, ::-1],
+                        scalar=rstd[:, 0:1],
+                        in1=rot[:, t, tbl, :].rearrange("p (j e) -> p j e", e=2).unsqueeze(1).to_broadcast([P, 4, 64, 2]),
+                        op0=ALU.mult,
+                        op1=ALU.mult,
+                    )
+            res = outp.tile([P, DM], F32, name="res")
+            nc.gpsimd.tensor_tensor(out=res[:], in0=prod[:, 0, :], in1=prod[:, 1, :], op=ALU.add)
+            nc.sync.dma_start(out=outs[hf][t * P : (t + 1) * P, :], in_=res[:])
+
+        for pair in range(4):
+            prep_w(0, pair)
+            load_w(1, pair)
+            prep_x(0, pair)
+            if pair == 1:
+                setup_gain_bias()
+
+        steps = [(c, hf, 0, FRAME) for c in (0, 1, 2) for hf in (0, 1)]
+        steps += [(3, 0, 0, FRAME), (3, 1, 0, 256), (3, 1, 256, 128), (3, 1, 384, 128)]
+
+        prev = None
+        for s, (c, hf, t0, n) in enumerate(steps):
+            vT = tpose.tile([P, NH, n], F32, name="vT")
+            sqT = tpose.tile([P, NH, n], F32, name="sqT")
+            units = 0 if prev is None else prev[3] // P
+            sqacc = None
+            if units > 0:
+                sqacc = psum.tile([P, FRAME], F32, name="sqacc", tag="bank")
+            for part in range(4):
+                project(c, hf, t0, n, 2 * part, vT, sqT)
+                project(c, hf, t0, n, 2 * part + 1, vT, sqT)
+                if units > 0 and part % (4 // units) == 0:
+                    finish_unit(prev[0], prev[1], prev[2], part // (4 // units), prev[4], prev[5], sqacc)
+                if s == 0:
+                    if part == 0:
+                        setup_rot()
+                    prep_w(1, part)
+                    for i in range(3 * part, 3 * part + 3):
+                        prep_x(1 + i // 4, i % 4)
+            prev = (c, hf, t0, n, vT, sqT)
+        sqacc = psum.tile([P, FRAME], F32, name="sqacc", tag="bank")
+        for a in range(prev[3] // P):
+            finish_unit(prev[0], prev[1], prev[2], a, prev[4], prev[5], sqacc)

@@ -81,7 +81,12 @@ def tile_causalwanselfattention_pa_kernel(
 
         def load_x(c):
             t = xbp.tile([P, 4, K], U8, name="xb")
-            nc.sync.dma_start(out=t[:], in_=xb_dram[c * FRAME : (c + 1) * FRAME, :].rearrange("(a p) k -> p a k", p=P))
+            rows = xb_dram[c * FRAME : (c + 1) * FRAME, :].rearrange("(a p) k -> p a k", p=P)
+            if c == 0:
+                nc.sync.dma_start(out=t[:, 0:1, :], in_=rows[:, 0:1, :])
+                nc.sync.dma_start(out=t[:, 1:4, :], in_=rows[:, 1:4, :])
+            else:
+                nc.sync.dma_start(out=t[:], in_=rows)
             xb[c] = t
 
         def load_w(hf, pair):
@@ -91,9 +96,9 @@ def tile_causalwanselfattention_pa_kernel(
             )
             wb[(hf, pair)] = t
 
-        load_w(0, 0)
         nc.sync.dma_start(out=xs_bc[:], in_=x_scale.rearrange("a b k -> (a b k)").partition_broadcast(P))
         load_x(0)
+        load_w(0, 0)
         load_w(0, 1)
         load_small()
         load_w(0, 2)
@@ -116,24 +121,26 @@ def tile_causalwanselfattention_pa_kernel(
         def setup_gain_bias():
             gb_ps = psum.tile([P, P], BF16, name="gb_ps", tag="bank")
             nc.tensor.transpose(gb_ps[:], gbrow[:], ident_bf[:])
-            nc.vector.tensor_copy(out=gbT[:], in_=gb_ps[:, 0:32])
-            nc.vector.tensor_tensor(out=gbp[:], in0=gbT[:, 0:16], in1=gbT[:, 16:32], op=ALU.mult)
-            nc.vector.tensor_scalar(out=b32[:], in0=gbT[:, 16:32], scalar1=1.0 / ROOT_DM, scalar2=None, op0=ALU.mult)
+            nc.scalar.copy(out=gbT[:], in_=gb_ps[:, 0:32])
+            nc.gpsimd.tensor_tensor(out=gbp[:], in0=gbT[:, 0:16], in1=gbT[:, 16:32], op=ALU.mult)
+            nc.gpsimd.tensor_scalar(
+                out=b32[:], in0=gbT[:, 16:32], scalar1=1.0 / ROOT_DM, scalar2=0.0, op0=ALU.mult, op1=ALU.add
+            )
 
         def setup_rot():
             rows0 = 4 * NF
             cols0 = 4 * NF + 4 * NR
-            nc.vector.tensor_copy(
+            nc.gpsimd.tensor_copy(
                 out=ang[:, 0:rows0].rearrange("p (f j) -> p f j", f=4),
                 in_=fr16[:, FIRST_FRAME_ROW : FIRST_FRAME_ROW + 4, 0:NF],
             )
             for q in range(4):
                 quad = slice(32 * q, 32 * q + 32)
-                nc.vector.tensor_copy(
+                nc.gpsimd.tensor_copy(
                     out=ang[quad, rows0:cols0].rearrange("p (f j) -> p f j", f=4),
                     in_=fr16[quad, q:16:4, NF : NF + NR],
                 )
-            nc.vector.tensor_copy(out=ang[:, cols0:NANG], in_=fcol[:, NF + NR : 64])
+            nc.gpsimd.tensor_copy(out=ang[:, cols0:NANG], in_=fcol[:, NF + NR : 64])
 
             nc.scalar.activation(out=trig[:, 1, :, 0], in_=ang[:], func=ACT.Sin, scale=-1.0)
             nc.scalar.activation(out=trig[:, 1, :, 1], in_=ang[:], func=ACT.Sin)
@@ -222,7 +229,7 @@ def tile_causalwanselfattention_pa_kernel(
             nc.scalar.activation(out=vT[:, j, :], in_=acc[:], func=ACT.Identity, scale=gbT[:, col], bias=gbp[:, col])
             nc.scalar.activation(out=sqT[:, j, :], in_=acc[:], func=ACT.Square, scale=1.0 / ROOT_DM, bias=b32[:, col])
 
-        def finish_unit(c, hf, t0, a, vT, sqT, sqacc):
+        def finish_unit(c, hf, t0, a, vT, sqT, sqacc, last=False):
             t = 4 * c + t0 // P + a
             tok = slice(a * P, (a + 1) * P)
             for j in range(NH):
@@ -253,13 +260,19 @@ def tile_causalwanselfattention_pa_kernel(
                         op1=ALU.mult,
                     )
             res = outp.tile([P, DM], F32, name="res")
-            nc.gpsimd.tensor_tensor(out=res[:], in0=prod[:, 0, :], in1=prod[:, 1, :], op=ALU.add)
-            nc.sync.dma_start(out=outs[hf][t * P : (t + 1) * P, :], in_=res[:])
+            if last:
+                for b, eng in enumerate((nc.gpsimd, nc.vector)):
+                    half = slice(b * BANK, (b + 1) * BANK)
+                    eng.tensor_tensor(out=res[:, half], in0=prod[:, 0, half], in1=prod[:, 1, half], op=ALU.add)
+                    nc.sync.dma_start(out=outs[hf][t * P : (t + 1) * P, half], in_=res[:, half])
+            else:
+                nc.gpsimd.tensor_tensor(out=res[:], in0=prod[:, 0, :], in1=prod[:, 1, :], op=ALU.add)
+                nc.sync.dma_start(out=outs[hf][t * P : (t + 1) * P, :], in_=res[:])
 
         for pair in range(4):
+            prep_x(0, pair)
             prep_w(0, pair)
             load_w(1, pair)
-            prep_x(0, pair)
             if pair == 1:
                 setup_gain_bias()
 
@@ -288,4 +301,4 @@ def tile_causalwanselfattention_pa_kernel(
             prev = (c, hf, t0, n, vT, sqT)
         sqacc = psum.tile([P, FRAME], F32, name="sqacc", tag="bank")
         for a in range(prev[3] // P):
-            finish_unit(prev[0], prev[1], prev[2], a, prev[4], prev[5], sqacc)
+            finish_unit(prev[0], prev[1], prev[2], a, prev[4], prev[5], sqacc, last=True)

@@ -44,14 +44,14 @@ def tile_causalwanselfattention_pa_kernel(
 
     with ExitStack() as ctx:
         const = ctx.enter_context(tc.tile_pool(name="const", bufs=1))
-        xbp = ctx.enter_context(tc.tile_pool(name="xbp", bufs=4))
+        xbp = ctx.enter_context(tc.tile_pool(name="xbp", bufs=3))
         xwp = ctx.enter_context(tc.tile_pool(name="xwp", bufs=3))
         xgp = ctx.enter_context(tc.tile_pool(name="xgp", bufs=2))
         wbp = ctx.enter_context(tc.tile_pool(name="wbp", bufs=4))
         wgp = ctx.enter_context(tc.tile_pool(name="wgp", bufs=3))
         tpose = ctx.enter_context(tc.tile_pool(name="tpose", bufs=2))
         mmp = ctx.enter_context(tc.tile_pool(name="mmp", bufs=3))
-        outp = ctx.enter_context(tc.tile_pool(name="outp", bufs=3))
+        outp = ctx.enter_context(tc.tile_pool(name="outp", bufs=5))
         small = ctx.enter_context(tc.tile_pool(name="small", bufs=4))
         psum = ctx.enter_context(tc.psum_pool(name="psum", bufs=8))
 
@@ -105,7 +105,6 @@ def tile_causalwanselfattention_pa_kernel(
         load_w(0, 3)
         load_x(1)
         load_x(2)
-        load_x(3)
 
         ident_bf = const.tile([P, P], BF16, name="ident_bf")
         make_identity(nc, ident_bf[:])
@@ -275,6 +274,7 @@ def tile_causalwanselfattention_pa_kernel(
             load_w(1, pair)
             if pair == 1:
                 setup_gain_bias()
+        load_x(3)
 
         steps = [(c, hf, 0, FRAME) for c in (0, 1, 2) for hf in (0, 1)]
         steps += [(3, 0, 0, FRAME), (3, 1, 0, 256), (3, 1, 256, 128), (3, 1, 384, 128)]

@@ -46,12 +46,12 @@ def tile_causalwanselfattention_pa_kernel(
         const = ctx.enter_context(tc.tile_pool(name="const", bufs=1))
         xbp = ctx.enter_context(tc.tile_pool(name="xbp", bufs=3))
         xwp = ctx.enter_context(tc.tile_pool(name="xwp", bufs=3))
-        xgp = ctx.enter_context(tc.tile_pool(name="xgp", bufs=2))
+        xgp = ctx.enter_context(tc.tile_pool(name="xgp", bufs=3))
         wbp = ctx.enter_context(tc.tile_pool(name="wbp", bufs=4))
         wgp = ctx.enter_context(tc.tile_pool(name="wgp", bufs=3))
         tpose = ctx.enter_context(tc.tile_pool(name="tpose", bufs=2))
         mmp = ctx.enter_context(tc.tile_pool(name="mmp", bufs=3))
-        outp = ctx.enter_context(tc.tile_pool(name="outp", bufs=5))
+        outp = ctx.enter_context(tc.tile_pool(name="outp", bufs=3))
         small = ctx.enter_context(tc.tile_pool(name="small", bufs=4))
         psum = ctx.enter_context(tc.psum_pool(name="psum", bufs=8))
 
@@ -201,14 +201,17 @@ def tile_causalwanselfattention_pa_kernel(
 
         xg = {}
 
+        def quantise_x(c):
+            quantise(xg[c][:], xq[:, c, :, :], xsc[:, c, :, :])
+
         def prep_x(c, a):
             if a == 0:
                 xg[c] = xgp.tile([P, 2, FRAME, 2], F32, name="xg", align_bytes=64)
             xw = xwp.tile([P, K], BF16, name="xw")
             nc.vector.tensor_tensor(out=xw[:], in0=xb[c][:, a, :].bitcast(FP8), in1=xs_bc[:], op=ALU.mult)
             k_to_partitions(xw[:].bitcast(F32), xg[c][:, :, a * P : (a + 1) * P, :])
-            if a == 3:
-                quantise(xg[c][:], xq[:, c, :, :], xsc[:, c, :, :])
+            if a == 3 and c < 2:
+                quantise_x(c)
 
         def project(c, hf, t0, n, j, vT, sqT):
             acc = psum.tile([P, n], F32, name="acc", tag="bank")
@@ -298,6 +301,8 @@ def tile_causalwanselfattention_pa_kernel(
                     prep_w(1, part)
                     for i in range(3 * part, 3 * part + 3):
                         prep_x(1 + i // 4, i % 4)
+                if s in (2, 4) and part == 1:
+                    quantise_x(s // 2 + 1)
             prev = (c, hf, t0, n, vT, sqT)
         sqacc = psum.tile([P, FRAME], F32, name="sqacc", tag="bank")
         for a in range(prev[3] // P):

@@ -115,7 +115,7 @@ def tile_causalwanselfattention_pa_kernel(
         ang = const.tile([P, NANG], F32, name="ang")
         trig = const.tile([P, 2, NANG, 2], F32, name="trig")
         absang = const.tile([P, NANG], F32, name="absang")
-        rot = const.tile([P, 16, 2, P], F32, name="rot")
+        rot = const.tile([P, 16, 2 * P], F32, name="rot")
 
         def setup_gain_bias():
             gb_ps = psum.tile([P, P], BF16, name="gb_ps", tag="bank")
@@ -141,8 +141,8 @@ def tile_causalwanselfattention_pa_kernel(
                 )
             nc.gpsimd.tensor_copy(out=ang[:, cols0:NANG], in_=fcol[:, NF + NR : 64])
 
-            nc.scalar.activation(out=trig[:, 1, :, 0], in_=ang[:], func=ACT.Sin, scale=-1.0)
-            nc.scalar.activation(out=trig[:, 1, :, 1], in_=ang[:], func=ACT.Sin)
+            nc.scalar.activation(out=trig[:, 1, :, 0], in_=ang[:], func=ACT.Sin)
+            nc.scalar.activation(out=trig[:, 1, :, 1], in_=ang[:], func=ACT.Sin, scale=-1.0)
             nc.scalar.activation(out=absang[:], in_=ang[:], func=ACT.Abs)
             nc.scalar.activation(
                 out=trig[:, 0, :, :],
@@ -154,24 +154,24 @@ def tile_causalwanselfattention_pa_kernel(
             nc.scalar.activation(out=warm[:, 1:2], in_=trig[:, 0, 0:1, 0], func=ACT.Abs_reciprocal_sqrt, bias=2.0)
 
             def spread(dst, a0, n, reps):
-                src = trig[:, :, a0 : a0 + n, :].rearrange("p t j e -> p t (j e)")
+                src = trig[:, :, a0 : a0 + n, :].rearrange("p t j e -> p (j e) t")
                 nc.gpsimd.tensor_scalar(
-                    out=dst,
-                    in0=src.unsqueeze(1).to_broadcast([P, reps, 2, 2 * n]),
+                    out=dst.rearrange("p r (c t) -> p r c t", t=2),
+                    in0=src.unsqueeze(1).to_broadcast([P, reps, 2 * n, 2]),
                     scalar1=1.0,
                     scalar2=0.0,
                     op0=ALU.mult,
                     op1=ALU.add,
                 )
 
-            row_ch = slice(2 * NF, 2 * (NF + NR))
-            spread(rot[:, 0:4, :, 0 : 2 * NF], 0, NF, 4)
-            spread(rot[:, 0:16:4, :, row_ch], rows0, NR, 4)
-            spread(rot[:, :, :, 2 * (NF + NR) : P], cols0, NCOL, 16)
+            row_ch = slice(4 * NF, 4 * (NF + NR))
+            spread(rot[:, 0:4, 0 : 4 * NF], 0, NF, 4)
+            spread(rot[:, 0:16:4, row_ch], rows0, NR, 4)
+            spread(rot[:, :, 4 * (NF + NR) : 2 * P], cols0, NCOL, 16)
             for f in range(1, 4):
-                spread(rot[:, f:16:4, :, row_ch], rows0 + f * NR, NR, 4)
+                spread(rot[:, f:16:4, row_ch], rows0 + f * NR, NR, 4)
             for f in range(1, 4):
-                spread(rot[:, 4 * f : 4 * f + 4, :, 0 : 2 * NF], f * NF, NF, 4)
+                spread(rot[:, 4 * f : 4 * f + 4, 0 : 4 * NF], f * NF, NF, 4)
 
         wq = const.tile([P, 2, 4, 2, PAIR], U32, name="wq", align_bytes=64)
         wsc = const.tile([P, 2, 4, 2, PAIR], U8, name="wsc", align_bytes=64)
@@ -249,26 +249,27 @@ def tile_causalwanselfattention_pa_kernel(
             nc.scalar.activation(out=junk[:], in_=sqacc[:, tok], func=ACT.Copy, accum_out=ms[:])
             rstd = small.tile([P, 1], F32, name="rstd")
             nc.scalar.activation(out=rstd[:], in_=ms[:], func=ACT.Abs_reciprocal_sqrt, bias=EPS)
-            prod = mmp.tile([P, 2, DM], F32, name="prod")
+            prod = mmp.tile([P, DM, 2], F32, name="prod")
             for b in range(2):
-                for tbl in range(2):
-                    pairs = banks[b][:].rearrange("p (h j e) -> p h j e", h=4, e=2)
-                    nc.vector.scalar_tensor_tensor(
-                        out=prod[:, tbl, b * BANK : (b + 1) * BANK].rearrange("p (h j e) -> p h j e", h=4, e=2),
-                        in0=pairs if tbl == 0 else pairs[:, :, :, ::-1],
-                        scalar=rstd[:, 0:1],
-                        in1=rot[:, t, tbl, :].rearrange("p (j e) -> p j e", e=2).unsqueeze(1).to_broadcast([P, 4, 64, 2]),
-                        op0=ALU.mult,
-                        op1=ALU.mult,
-                    )
+                nc.vector.scalar_tensor_tensor(
+                    out=prod[:, b * BANK : (b + 1) * BANK, :].rearrange("p (h c) t -> p h c t", h=4),
+                    in0=banks[b][:].rearrange("p (h c) -> p h c", h=4).unsqueeze(3).to_broadcast([P, 4, P, 2]),
+                    scalar=rstd[:, 0:1],
+                    in1=rot[:, t, :].rearrange("p (c t) -> p c t", t=2).unsqueeze(1).to_broadcast([P, 4, P, 2]),
+                    op0=ALU.mult,
+                    op1=ALU.mult,
+                )
             res = outp.tile([P, DM], F32, name="res")
+            pairs = prod[:].rearrange("p (j e) t -> p j e t", e=2)
+            outpairs = res[:].rearrange("p (j e) -> p j e", e=2)
             if last:
                 for b, eng in enumerate((nc.gpsimd, nc.vector)):
                     half = slice(b * BANK, (b + 1) * BANK)
-                    eng.tensor_tensor(out=res[:, half], in0=prod[:, 0, half], in1=prod[:, 1, half], op=ALU.add)
+                    hp = slice(b * BANK // 2, (b + 1) * BANK // 2)
+                    eng.tensor_tensor(out=outpairs[:, hp, :], in0=pairs[:, hp, :, 0], in1=pairs[:, hp, ::-1, 1], op=ALU.add)
                     nc.sync.dma_start(out=outs[hf][t * P : (t + 1) * P, half], in_=res[:, half])
             else:
-                nc.gpsimd.tensor_tensor(out=res[:], in0=prod[:, 0, :], in1=prod[:, 1, :], op=ALU.add)
+                nc.gpsimd.tensor_tensor(out=outpairs, in0=pairs[:, :, :, 0], in1=pairs[:, :, ::-1, 1], op=ALU.add)
                 nc.sync.dma_start(out=outs[hf][t * P : (t + 1) * P, :], in_=res[:])
 
         for pair in range(4):

@@ -63,18 +63,13 @@ def tile_causalwanselfattention_pa_kernel(
         nc.vector.memset(warm[:], 0.0)
         nc.scalar.activation(out=warm[:, 1:2], in_=warm[:, 0:1], func=ACT.Sin)
         xs_bc = const.tile([P, K], F32, name="xs_bc")
-        fcol = const.tile([P, 64], BF16, name="fcol")
-        fr16 = const.tile([P, 16, 64], BF16, name="fr16")
+        frows = const.tile([P, 64], BF16, name="frows")
+        nc.vector.memset(frows[:], 0.0)
 
         def load_small():
+            nc.sync.dma_start(out=frows[0:32, :], in_=freqs[0:32, :])
             for i, vec in enumerate((gq, gk, bq, bk)):
                 nc.sync.dma_start(out=gbrow[8 * i : 8 * i + 8, :], in_=vec.rearrange("(j p) -> j p", p=P))
-            for q in range(4):
-                nc.sync.dma_start(out=fcol[32 * q : 32 * q + 32, :], in_=freqs[0:32, :])
-            nc.sync.dma_start(
-                out=fr16[:].rearrange("p r c -> p (r c)"),
-                in_=freqs[0:16, :].rearrange("r c -> (r c)").partition_broadcast(P),
-            )
 
         xb = {}
         wb = {}
@@ -112,7 +107,7 @@ def tile_causalwanselfattention_pa_kernel(
         gbT = const.tile([P, 32], F32, name="gbT")
         gbp = const.tile([P, 16], F32, name="gbp")
         b32 = const.tile([P, 16], F32, name="b32")
-        ang = const.tile([P, NANG], F32, name="ang")
+        pick = const.tile([P, 20, 32], BF16, name="pick")
         trig = const.tile([P, 2, NANG, 2], F32, name="trig")
         absang = const.tile([P, NANG], F32, name="absang")
         rot = const.tile([P, 16, 2 * P], F32, name="rot")
@@ -129,17 +124,27 @@ def tile_causalwanselfattention_pa_kernel(
         def setup_rot():
             rows0 = 4 * NF
             cols0 = 4 * NF + 4 * NR
-            nc.gpsimd.tensor_copy(
-                out=ang[:, 0:rows0].rearrange("p (f j) -> p f j", f=4),
-                in_=fr16[:, FIRST_FRAME_ROW : FIRST_FRAME_ROW + 4, 0:NF],
-            )
-            for q in range(4):
-                quad = slice(32 * q, 32 * q + 32)
-                nc.gpsimd.tensor_copy(
-                    out=ang[quad, rows0:cols0].rearrange("p (f j) -> p f j", f=4),
-                    in_=fr16[quad, q:16:4, NF : NF + NR],
+            nc.gpsimd.tensor_copy(out=pick[:, 0:16, :], in_=ident_bf[:, 0:16].unsqueeze(2).to_broadcast([P, 16, 32]))
+            nc.gpsimd.tensor_copy(out=pick[:, 16:20, :], in_=ident_bf[:, 0:32].unsqueeze(1).to_broadcast([P, 4, 32]))
+            ang = psum.tile([P, NANG], F32, name="ang", tag="bank")
+            for f in range(4):
+                row = FIRST_FRAME_ROW + f
+                nc.tensor.matmul(
+                    out=ang[:, f * NF : (f + 1) * NF],
+                    lhsT=ident_bf[:, row : row + 1].to_broadcast([P, P]),
+                    rhs=frows[:, 0:NF],
+                    start=True,
+                    stop=True,
                 )
-            nc.gpsimd.tensor_copy(out=ang[:, cols0:NANG], in_=fcol[:, NF + NR : 64])
+            for q in range(5):
+                c0, n, a = (NF, NR, rows0 + q * NR) if q < 4 else (NF + NR, NCOL, cols0)
+                nc.tensor.matmul(
+                    out=ang[:, a : a + n],
+                    lhsT=pick[:, 4 * q : 4 * q + 4, :].rearrange("p r c -> p (r c)"),
+                    rhs=frows[:, c0 : c0 + n],
+                    start=True,
+                    stop=True,
+                )
 
             nc.scalar.activation(out=trig[:, 1, :, 0], in_=ang[:], func=ACT.Sin)
             nc.scalar.activation(out=trig[:, 1, :, 1], in_=ang[:], func=ACT.Sin, scale=-1.0)
@@ -278,7 +283,10 @@ def tile_causalwanselfattention_pa_kernel(
             load_w(1, pair)
             if pair == 1:
                 setup_gain_bias()
+                setup_rot()
         load_x(3)
+        prep_x(1, 0)
+        prep_x(1, 1)
 
         steps = [(c, hf, 0, FRAME) for c in (0, 1, 2) for hf in (0, 1)]
         steps += [(3, 0, 0, FRAME), (3, 1, 0, 256), (3, 1, 256, 128), (3, 1, 384, 128)]
@@ -297,10 +305,8 @@ def tile_causalwanselfattention_pa_kernel(
                 if units > 0 and part % (4 // units) == 0:
                     finish_unit(prev[0], prev[1], prev[2], part // (4 // units), prev[4], prev[5], sqacc)
                 if s == 0:
-                    if part == 0:
-                        setup_rot()
                     prep_w(1, part)
-                    for i in range(3 * part, 3 * part + 3):
+                    for i in range((4, 7, 10, 12)[part - 1] if part > 0 else 2, (4, 7, 10, 12)[part]):
                         prep_x(1 + i // 4, i % 4)
                 if s in (2, 4) and part == 1:
                     quantise_x(s // 2 + 1)

@@ -103,14 +103,16 @@ def tile_causalwanselfattention_pa_kernel(
 
         ident_bf = const.tile([P, P], BF16, name="ident_bf")
         make_identity(nc, ident_bf[:])
+        pick = const.tile([P, 20, 32], BF16, name="pick")
+        nc.vector.tensor_copy(out=pick[:, 0:16, :], in_=ident_bf[:, 0:16].unsqueeze(2).to_broadcast([P, 16, 32]))
+        nc.vector.tensor_copy(out=pick[:, 16:20, :], in_=ident_bf[:, 0:32].unsqueeze(1).to_broadcast([P, 4, 32]))
 
         gbT = const.tile([P, 32], F32, name="gbT")
         gbp = const.tile([P, 16], F32, name="gbp")
         b32 = const.tile([P, 16], F32, name="b32")
-        pick = const.tile([P, 20, 32], BF16, name="pick")
         trig = const.tile([P, 2, NANG, 2], F32, name="trig")
         absang = const.tile([P, NANG], F32, name="absang")
-        rot = const.tile([P, 16, 2 * P], F32, name="rot")
+        rot = const.tile([P, 2, 4, 2 * P], F32, name="rot")
 
         def setup_gain_bias():
             gb_ps = psum.tile([P, P], BF16, name="gb_ps", tag="bank")
@@ -121,11 +123,23 @@ def tile_causalwanselfattention_pa_kernel(
                 out=b32[:], in0=gbT[:, 16:32], scalar1=1.0 / ROOT_DM, scalar2=0.0, op0=ALU.mult, op1=ALU.add
             )
 
+        def spread(dst, a0, n, reps):
+            src = trig[:, :, a0 : a0 + n, :].rearrange("p t j e -> p (j e) t")
+            nc.gpsimd.tensor_scalar(
+                out=dst.rearrange("p r (c t) -> p r c t", t=2),
+                in0=src.unsqueeze(1).to_broadcast([P, reps, 2 * n, 2]),
+                scalar1=1.0,
+                scalar2=0.0,
+                op0=ALU.mult,
+                op1=ALU.add,
+            )
+
+        def spread_frame(f):
+            spread(rot[:, f % 2, :, 0 : 4 * NF], f * NF, NF, 4)
+
         def setup_rot():
             rows0 = 4 * NF
             cols0 = 4 * NF + 4 * NR
-            nc.gpsimd.tensor_copy(out=pick[:, 0:16, :], in_=ident_bf[:, 0:16].unsqueeze(2).to_broadcast([P, 16, 32]))
-            nc.gpsimd.tensor_copy(out=pick[:, 16:20, :], in_=ident_bf[:, 0:32].unsqueeze(1).to_broadcast([P, 4, 32]))
             ang = psum.tile([P, NANG], F32, name="ang", tag="bank")
             for f in range(4):
                 row = FIRST_FRAME_ROW + f
@@ -158,25 +172,13 @@ def tile_causalwanselfattention_pa_kernel(
             )
             nc.scalar.activation(out=warm[:, 1:2], in_=trig[:, 0, 0:1, 0], func=ACT.Abs_reciprocal_sqrt, bias=2.0)
 
-            def spread(dst, a0, n, reps):
-                src = trig[:, :, a0 : a0 + n, :].rearrange("p t j e -> p (j e) t")
-                nc.gpsimd.tensor_scalar(
-                    out=dst.rearrange("p r (c t) -> p r c t", t=2),
-                    in0=src.unsqueeze(1).to_broadcast([P, reps, 2 * n, 2]),
-                    scalar1=1.0,
-                    scalar2=0.0,
-                    op0=ALU.mult,
-                    op1=ALU.add,
-                )
-
             row_ch = slice(4 * NF, 4 * (NF + NR))
-            spread(rot[:, 0:4, 0 : 4 * NF], 0, NF, 4)
-            spread(rot[:, 0:16:4, row_ch], rows0, NR, 4)
-            spread(rot[:, :, 4 * (NF + NR) : 2 * P], cols0, NCOL, 16)
-            for f in range(1, 4):
-                spread(rot[:, f:16:4, row_ch], rows0 + f * NR, NR, 4)
-            for f in range(1, 4):
-                spread(rot[:, 4 * f : 4 * f + 4, 0 : 4 * NF], f * NF, NF, 4)
+            spread_frame(0)
+            spread(rot[:, :, 0, row_ch], rows0, NR, 2)
+            spread(rot[:, :, :, 4 * (NF + NR) : 2 * P].rearrange("p f q c -> p (f q) c"), cols0, NCOL, 8)
+            for q in range(1, 4):
+                spread(rot[:, :, q, row_ch], rows0 + q * NR, NR, 2)
+            spread_frame(1)
 
         wq = const.tile([P, 2, 4, 2, PAIR], U32, name="wq", align_bytes=64)
         wsc = const.tile([P, 2, 4, 2, PAIR], U8, name="wsc", align_bytes=64)
@@ -260,7 +262,7 @@ def tile_causalwanselfattention_pa_kernel(
                     out=prod[:, b * BANK : (b + 1) * BANK, :].rearrange("p (h c) t -> p h c t", h=4),
                     in0=banks[b][:].rearrange("p (h c) -> p h c", h=4).unsqueeze(3).to_broadcast([P, 4, P, 2]),
                     scalar=rstd[:, 0:1],
-                    in1=rot[:, t, :].rearrange("p (c t) -> p c t", t=2).unsqueeze(1).to_broadcast([P, 4, P, 2]),
+                    in1=rot[:, (t // 4) % 2, t % 4, :].rearrange("p (c t) -> p c t", t=2).unsqueeze(1).to_broadcast([P, 4, P, 2]),
                     op0=ALU.mult,
                     op1=ALU.mult,
                 )
@@ -310,6 +312,8 @@ def tile_causalwanselfattention_pa_kernel(
                         prep_x(1 + i // 4, i % 4)
                 if s in (2, 4) and part == 1:
                     quantise_x(s // 2 + 1)
+                if s in (3, 5) and part == 0:
+                    spread_frame(s // 2 + 1)
             prev = (c, hf, t0, n, vT, sqT)
         sqacc = psum.tile([P, FRAME], F32, name="sqacc", tag="bank")
         for a in range(prev[3] // P):

@@ -95,9 +95,9 @@ def tile_causalwanselfattention_pa_kernel(
         load_x(0)
         load_w(0, 0)
         load_w(0, 1)
-        load_small()
         load_w(0, 2)
         load_w(0, 3)
+        load_small()
         load_x(1)
         load_x(2)
 
@@ -238,12 +238,13 @@ def tile_causalwanselfattention_pa_kernel(
             nc.scalar.activation(out=vT[:, j, :], in_=acc[:], func=ACT.Identity, scale=gbT[:, col], bias=gbp[:, col])
             nc.scalar.activation(out=sqT[:, j, :], in_=acc[:], func=ACT.Square, scale=1.0 / ROOT_DM, bias=b32[:, col])
 
-        def finish_unit(c, hf, t0, a, vT, sqT, sqacc, last=False):
+        def finish_unit(c, hf, t0, a, vT, sqT, last=False):
             t = 4 * c + t0 // P + a
             tok = slice(a * P, (a + 1) * P)
+            sqacc = psum.tile([P, P], F32, name="sqacc", tag="bank")
             for j in range(NH):
                 nc.tensor.matmul(
-                    out=sqacc[:, tok], lhsT=sqT[:, j, tok], rhs=ident[:], is_transpose=True, start=(j == 0), stop=(j == NH - 1)
+                    out=sqacc[:], lhsT=sqT[:, j, tok], rhs=ident[:], is_transpose=True, start=(j == 0), stop=(j == NH - 1)
                 )
             banks = []
             for b in range(2):
@@ -253,7 +254,7 @@ def tile_causalwanselfattention_pa_kernel(
                 banks.append(vb)
             junk = small.tile([P, P], BF16, name="junk")
             ms = small.tile([P, 1], F32, name="ms")
-            nc.scalar.activation(out=junk[:], in_=sqacc[:, tok], func=ACT.Copy, accum_out=ms[:])
+            nc.scalar.activation(out=junk[:], in_=sqacc[:], func=ACT.Copy, accum_out=ms[:])
             rstd = small.tile([P, 1], F32, name="rstd")
             nc.scalar.activation(out=rstd[:], in_=ms[:], func=ACT.Abs_reciprocal_sqrt, bias=EPS)
             prod = mmp.tile([P, DM, 2], F32, name="prod")
@@ -298,14 +299,11 @@ def tile_causalwanselfattention_pa_kernel(
             vT = tpose.tile([P, NH, n], F32, name="vT")
             sqT = tpose.tile([P, NH, n], F32, name="sqT")
             units = 0 if prev is None else prev[3] // P
-            sqacc = None
-            if units > 0:
-                sqacc = psum.tile([P, FRAME], F32, name="sqacc", tag="bank")
             for part in range(4):
                 project(c, hf, t0, n, 2 * part, vT, sqT)
                 project(c, hf, t0, n, 2 * part + 1, vT, sqT)
                 if units > 0 and part % (4 // units) == 0:
-                    finish_unit(prev[0], prev[1], prev[2], part // (4 // units), prev[4], prev[5], sqacc)
+                    finish_unit(prev[0], prev[1], prev[2], part // (4 // units), prev[4], prev[5])
                 if s == 0:
                     prep_w(1, part)
                     for i in range((4, 7, 10, 12)[part - 1] if part > 0 else 2, (4, 7, 10, 12)[part]):
@@ -315,6 +313,5 @@ def tile_causalwanselfattention_pa_kernel(
                 if s in (3, 5) and part == 0:
                     spread_frame(s // 2 + 1)
             prev = (c, hf, t0, n, vT, sqT)
-        sqacc = psum.tile([P, FRAME], F32, name="sqacc", tag="bank")
         for a in range(prev[3] // P):
-            finish_unit(prev[0], prev[1], prev[2], a, prev[4], prev[5], sqacc, last=True)
+            finish_unit(prev[0], prev[1], prev[2], a, prev[4], prev[5], last=True)

@@ -45,10 +45,10 @@ def tile_causalwanselfattention_pa_kernel(
     with ExitStack() as ctx:
         const = ctx.enter_context(tc.tile_pool(name="const", bufs=1))
         xbp = ctx.enter_context(tc.tile_pool(name="xbp", bufs=3))
-        xwp = ctx.enter_context(tc.tile_pool(name="xwp", bufs=3))
+        xwp = ctx.enter_context(tc.tile_pool(name="xwp", bufs=4))
         xgp = ctx.enter_context(tc.tile_pool(name="xgp", bufs=3))
         wbp = ctx.enter_context(tc.tile_pool(name="wbp", bufs=4))
-        wgp = ctx.enter_context(tc.tile_pool(name="wgp", bufs=3))
+        wgp = ctx.enter_context(tc.tile_pool(name="wgp", bufs=4))
         tpose = ctx.enter_context(tc.tile_pool(name="tpose", bufs=2))
         mmp = ctx.enter_context(tc.tile_pool(name="mmp", bufs=3))
         outp = ctx.enter_context(tc.tile_pool(name="outp", bufs=3))
@@ -185,13 +185,13 @@ def tile_causalwanselfattention_pa_kernel(
         xq = const.tile([P, NFRAME, 2, FRAME], U32, name="xq", align_bytes=64)
         xsc = const.tile([P, NFRAME, 2, FRAME], U8, name="xsc", align_bytes=64)
 
-        def k_to_partitions(words, dst):
+        def k_to_partitions(words, dst, copy):
             tp = psum.tile([P, BANK], F32, name="tp", tag="bank")
             for g in range(2):
                 for u in range(2):
                     i = 2 * g + u
                     nc.tensor.transpose(tp[:, i * P : (i + 1) * P], words[:, 256 * g + u : 256 * (g + 1) : 2], ident[:])
-            nc.scalar.copy(out=dst, in_=tp[:].rearrange("p (g u r) -> p g r u", g=2, u=2))
+            copy(out=dst, in_=tp[:].rearrange("p (g u r) -> p g r u", g=2, u=2))
 
         def quantise(grouped, codes, scales):
             nc.vector.quantize_mx(
@@ -203,7 +203,8 @@ def tile_causalwanselfattention_pa_kernel(
         def prep_w(hf, pair):
             wg = wgp.tile([P, 2, PAIR, 2], F32, name="wg", align_bytes=64)
             for hh in range(2):
-                k_to_partitions(wb[(hf, pair)][:, hh, :].bitcast(F32), wg[:, :, hh * P : (hh + 1) * P, :])
+                copy = nc.vector.tensor_copy if hf == 1 and 2 * pair + hh >= 5 else nc.scalar.copy
+                k_to_partitions(wb[(hf, pair)][:, hh, :].bitcast(F32), wg[:, :, hh * P : (hh + 1) * P, :], copy)
             quantise(wg[:], wq[:, hf, pair, :, :], wsc[:, hf, pair, :, :])
 
         xg = {}
@@ -216,7 +217,8 @@ def tile_causalwanselfattention_pa_kernel(
                 xg[c] = xgp.tile([P, 2, FRAME, 2], F32, name="xg", align_bytes=64)
             xw = xwp.tile([P, K], BF16, name="xw")
             nc.vector.tensor_tensor(out=xw[:], in0=xb[c][:, a, :].bitcast(FP8), in1=xs_bc[:], op=ALU.mult)
-            k_to_partitions(xw[:].bitcast(F32), xg[c][:, :, a * P : (a + 1) * P, :])
+            copy = nc.vector.tensor_copy if 4 * c + a >= 14 else nc.scalar.copy
+            k_to_partitions(xw[:].bitcast(F32), xg[c][:, :, a * P : (a + 1) * P, :], copy)
             if a == 3 and c < 2:
                 quantise_x(c)
 

@@ -219,7 +219,7 @@ def tile_causalwanselfattention_pa_kernel(
             nc.vector.tensor_tensor(out=xw[:], in0=xb[c][:, a, :].bitcast(FP8), in1=xs_bc[:], op=ALU.mult)
             copy = nc.vector.tensor_copy if 4 * c + a >= 14 else nc.scalar.copy
             k_to_partitions(xw[:].bitcast(F32), xg[c][:, :, a * P : (a + 1) * P, :], copy)
-            if a == 3 and c < 2:
+            if a == 3 and c == 0:
                 quantise_x(c)
 
         def project(c, hf, t0, n, j, vT, sqT):
@@ -240,11 +240,13 @@ def tile_causalwanselfattention_pa_kernel(
             nc.scalar.activation(out=vT[:, j, :], in_=acc[:], func=ACT.Identity, scale=gbT[:, col], bias=gbp[:, col])
             nc.scalar.activation(out=sqT[:, j, :], in_=acc[:], func=ACT.Square, scale=1.0 / ROOT_DM, bias=b32[:, col])
 
-        def finish_unit(c, hf, t0, a, vT, sqT, last=False):
+        def finish_unit(c, hf, t0, a, vT, sqT, paired, last=False):
             t = 4 * c + t0 // P + a
             tok = slice(a * P, (a + 1) * P)
             sqacc = psum.tile([P, P], F32, name="sqacc", tag="bank")
             for j in range(NH):
+                if j == 1 and paired:
+                    continue
                 nc.tensor.matmul(
                     out=sqacc[:], lhsT=sqT[:, j, tok], rhs=ident[:], is_transpose=True, start=(j == 0), stop=(j == NH - 1)
                 )
@@ -304,16 +306,18 @@ def tile_causalwanselfattention_pa_kernel(
             for part in range(4):
                 project(c, hf, t0, n, 2 * part, vT, sqT)
                 project(c, hf, t0, n, 2 * part + 1, vT, sqT)
+                if part == 0 and n == FRAME:
+                    nc.gpsimd.tensor_tensor(out=sqT[:, 0, :], in0=sqT[:, 0, :], in1=sqT[:, 1, :], op=ALU.add)
                 if units > 0 and part % (4 // units) == 0:
-                    finish_unit(prev[0], prev[1], prev[2], part // (4 // units), prev[4], prev[5])
+                    finish_unit(prev[0], prev[1], prev[2], part // (4 // units), prev[4], prev[5], prev[3] == FRAME)
                 if s == 0:
                     prep_w(1, part)
                     for i in range((4, 7, 10, 12)[part - 1] if part > 0 else 2, (4, 7, 10, 12)[part]):
                         prep_x(1 + i // 4, i % 4)
-                if s in (2, 4) and part == 1:
+                if s in (1, 2, 4) and part == 1:
                     quantise_x(s // 2 + 1)
                 if s in (3, 5) and part == 0:
                     spread_frame(s // 2 + 1)
             prev = (c, hf, t0, n, vT, sqT)
         for a in range(prev[3] // P):
-            finish_unit(prev[0], prev[1], prev[2], a, prev[4], prev[5], last=True)
+            finish_unit(prev[0], prev[1], prev[2], a, prev[4], prev[5], False, last=True)

from contextlib import ExitStack
import math

import concourse.mybir as mybir
from concourse.masks import make_identity

F32 = mybir.dt.float32
BF16 = mybir.dt.bfloat16
U32 = mybir.dt.uint32
U8 = mybir.dt.uint8
FP8 = mybir.dt.float8_e4m3fn
FP8X4 = mybir.dt.float8_e4m3fn_x4
ACT = mybir.ActivationFunctionType
ALU = mybir.AluOpType

P = 128
L = 2048
K = 1024
DM = 1024
NH = 8
FRAME = 512
NFRAME = L // FRAME
FIRST_FRAME_ROW = 2
EPS = 1e-6
NF, NR, NCOL = 22, 21, 21
NANG = 4 * NF + 4 * NR + NCOL
ROOT_DM = 32.0
BANK = 512
PAIR = 2 * P

FLOPS = 2 * L * K * 2 * DM


def tile_causalwanselfattention_pa_kernel(
    tc, x_bytes, x_scale, freqs, Wq, bq, Wk, bk, gq, gk, out_0, out_1
):
    nc = tc.nc
    xb_dram = x_bytes.rearrange("b l k -> (b l) k")
    outs = (
        out_0.rearrange("b l h d -> (b l) (h d)"),
        out_1.rearrange("b l h d -> (b l) (h d)"),
    )
    w_dram = (Wq, Wk)

    with ExitStack() as ctx:
        const = ctx.enter_context(tc.tile_pool(name="const", bufs=1))
        xbp = ctx.enter_context(tc.tile_pool(name="xbp", bufs=3))
        xwp = ctx.enter_context(tc.tile_pool(name="xwp", bufs=4))
        xgp = ctx.enter_context(tc.tile_pool(name="xgp", bufs=3))
        wbp = ctx.enter_context(tc.tile_pool(name="wbp", bufs=4))
        wgp = ctx.enter_context(tc.tile_pool(name="wgp", bufs=4))
        tpose = ctx.enter_context(tc.tile_pool(name="tpose", bufs=2))
        mmp = ctx.enter_context(tc.tile_pool(name="mmp", bufs=3))
        outp = ctx.enter_context(tc.tile_pool(name="outp", bufs=3))
        small = ctx.enter_context(tc.tile_pool(name="small", bufs=4))
        psum = ctx.enter_context(tc.psum_pool(name="psum", bufs=8))

        ident = const.tile([P, P], F32, name="ident")
        make_identity(nc, ident[:])
        gbrow = const.tile([P, P], BF16, name="gbrow")
        nc.vector.memset(gbrow[:], 0.0)
        warm = const.tile([P, 2], F32, name="warm")
        nc.vector.memset(warm[:], 0.0)
        nc.scalar.activation(out=warm[:, 1:2], in_=warm[:, 0:1], func=ACT.Sin)
        xs_bc = const.tile([P, K], F32, name="xs_bc")
        frows = const.tile([P, 64], BF16, name="frows")
        nc.vector.memset(frows[:], 0.0)

        def load_small():
            nc.sync.dma_start(out=frows[0:32, :], in_=freqs[0:32, :])
            for i, vec in enumerate((gq, gk, bq, bk)):
                nc.sync.dma_start(out=gbrow[8 * i : 8 * i + 8, :], in_=vec.rearrange("(j p) -> j p", p=P))

        xb = {}
        wb = {}

        def load_x(c):
            t = xbp.tile([P, 4, K], U8, name="xb")
            rows = xb_dram[c * FRAME : (c + 1) * FRAME, :].rearrange("(a p) k -> p a k", p=P)
            if c == 0:
                nc.sync.dma_start(out=t[:, 0:1, :], in_=rows[:, 0:1, :])
                nc.sync.dma_start(out=t[:, 1:4, :], in_=rows[:, 1:4, :])
            else:
                nc.sync.dma_start(out=t[:], in_=rows)
            xb[c] = t

        def load_w(hf, pair):
            t = wbp.tile([P, 2, K], BF16, name="wb")
            nc.sync.dma_start(
                out=t[:], in_=w_dram[hf][pair * PAIR : (pair + 1) * PAIR, :].rearrange("(a p) k -> p a k", p=P)
            )
            wb[(hf, pair)] = t

        nc.sync.dma_start(out=xs_bc[:], in_=x_scale.rearrange("a b k -> (a b k)").partition_broadcast(P))
        load_x(0)
        load_w(0, 0)
        load_w(0, 1)
        load_w(0, 2)
        load_w(0, 3)
        load_small()
        load_x(1)
        load_x(2)

        ident_bf = const.tile([P, P], BF16, name="ident_bf")
        make_identity(nc, ident_bf[:])
        pick = const.tile([P, 20, 32], BF16, name="pick")
        nc.vector.tensor_copy(out=pick[:, 0:16, :], in_=ident_bf[:, 0:16].unsqueeze(2).to_broadcast([P, 16, 32]))
        nc.vector.tensor_copy(out=pick[:, 16:20, :], in_=ident_bf[:, 0:32].unsqueeze(1).to_broadcast([P, 4, 32]))

        gbT = const.tile([P, 32], F32, name="gbT")
        gbp = const.tile([P, 16], F32, name="gbp")
        b32 = const.tile([P, 16], F32, name="b32")
        trig = const.tile([P, 2, NANG, 2], F32, name="trig")
        absang = const.tile([P, NANG], F32, name="absang")
        rot = const.tile([P, 2, 4, 2 * P], F32, name="rot")

        def setup_gain_bias():
            gb_ps = psum.tile([P, P], BF16, name="gb_ps", tag="bank")
            nc.tensor.transpose(gb_ps[:], gbrow[:], ident_bf[:])
            nc.scalar.copy(out=gbT[:], in_=gb_ps[:, 0:32])
            nc.gpsimd.tensor_tensor(out=gbp[:], in0=gbT[:, 0:16], in1=gbT[:, 16:32], op=ALU.mult)
            nc.gpsimd.tensor_scalar(
                out=b32[:], in0=gbT[:, 16:32], scalar1=1.0 / ROOT_DM, scalar2=0.0, op0=ALU.mult, op1=ALU.add
            )

        def spread(dst, a0, n, reps):
            src = trig[:, :, a0 : a0 + n, :].rearrange("p t j e -> p (j e) t")
            nc.gpsimd.tensor_scalar(
                out=dst.rearrange("p r (c t) -> p r c t", t=2),
                in0=src.unsqueeze(1).to_broadcast([P, reps, 2 * n, 2]),
                scalar1=1.0,
                scalar2=0.0,
                op0=ALU.mult,
                op1=ALU.add,
            )

        def spread_frame(f):
            spread(rot[:, f % 2, :, 0 : 4 * NF], f * NF, NF, 4)

        def setup_rot():
            rows0 = 4 * NF
            cols0 = 4 * NF + 4 * NR
            ang = psum.tile([P, NANG], F32, name="ang", tag="bank")
            for f in range(4):
                row = FIRST_FRAME_ROW + f
                nc.tensor.matmul(
                    out=ang[:, f * NF : (f + 1) * NF],
                    lhsT=ident_bf[:, row : row + 1].to_broadcast([P, P]),
                    rhs=frows[:, 0:NF],
                    start=True,
                    stop=True,
                )
            for q in range(5):
                c0, n, a = (NF, NR, rows0 + q * NR) if q < 4 else (NF + NR, NCOL, cols0)
                nc.tensor.matmul(
                    out=ang[:, a : a + n],
                    lhsT=pick[:, 4 * q : 4 * q + 4, :].rearrange("p r c -> p (r c)"),
                    rhs=frows[:, c0 : c0 + n],
                    start=True,
                    stop=True,
                )

            nc.scalar.activation(out=trig[:, 1, :, 0], in_=ang[:], func=ACT.Sin)
            nc.scalar.activation(out=trig[:, 1, :, 1], in_=ang[:], func=ACT.Sin, scale=-1.0)
            nc.scalar.activation(out=absang[:], in_=ang[:], func=ACT.Abs)
            nc.scalar.activation(
                out=trig[:, 0, :, :],
                in_=absang[:].unsqueeze(2).to_broadcast([P, NANG, 2]),
                func=ACT.Sin,
                scale=-1.0,
                bias=math.pi / 2.0,
            )
            nc.scalar.activation(out=warm[:, 1:2], in_=trig[:, 0, 0:1, 0], func=ACT.Abs_reciprocal_sqrt, bias=2.0)

            row_ch = slice(4 * NF, 4 * (NF + NR))
            spread_frame(0)
            spread(rot[:, :, 0, row_ch], rows0, NR, 2)
            spread(rot[:, :, :, 4 * (NF + NR) : 2 * P].rearrange("p f q c -> p (f q) c"), cols0, NCOL, 8)
            for q in range(1, 4):
                spread(rot[:, :, q, row_ch], rows0 + q * NR, NR, 2)
            spread_frame(1)

        wq = const.tile([P, 2, 4, 2, PAIR], U32, name="wq", align_bytes=64)
        wsc = const.tile([P, 2, 4, 2, PAIR], U8, name="wsc", align_bytes=64)
        xq = const.tile([P, NFRAME, 2, FRAME], U32, name="xq", align_bytes=64)
        xsc = const.tile([P, NFRAME, 2, FRAME], U8, name="xsc", align_bytes=64)

        def k_to_partitions(words, dst, copy):
            tp = psum.tile([P, BANK], F32, name="tp", tag="bank")
            for g in range(2):
                for u in range(2):
                    i = 2 * g + u
                    nc.tensor.transpose(tp[:, i * P : (i + 1) * P], words[:, 256 * g + u : 256 * (g + 1) : 2], ident[:])
            copy(out=dst, in_=tp[:].rearrange("p (g u r) -> p g r u", g=2, u=2))

        def quantise(grouped, codes, scales):
            nc.vector.quantize_mx(
                out=codes.rearrange("p g r -> p (g r)").bitcast(FP8X4),
                scales=scales.rearrange("p g r -> p (g r)"),
                in_=grouped.rearrange("p g r u -> p (g r u)").bitcast(BF16),
            )

        def prep_w(hf, pair):
            wg = wgp.tile([P, 2, PAIR, 2], F32, name="wg", align_bytes=64)
            for hh in range(2):
                copy = nc.vector.tensor_copy if hf == 1 and 2 * pair + hh >= 5 else nc.scalar.copy
                k_to_partitions(wb[(hf, pair)][:, hh, :].bitcast(F32), wg[:, :, hh * P : (hh + 1) * P, :], copy)
            quantise(wg[:], wq[:, hf, pair, :, :], wsc[:, hf, pair, :, :])

        xg = {}

        def quantise_x(c):
            quantise(xg[c][:], xq[:, c, :, :], xsc[:, c, :, :])

        def prep_x(c, a):
            if a == 0:
                xg[c] = xgp.tile([P, 2, FRAME, 2], F32, name="xg", align_bytes=64)
            xw = xwp.tile([P, K], BF16, name="xw")
            nc.vector.tensor_tensor(out=xw[:], in0=xb[c][:, a, :].bitcast(FP8), in1=xs_bc[:], op=ALU.mult)
            copy = nc.vector.tensor_copy if 4 * c + a >= 14 else nc.scalar.copy
            k_to_partitions(xw[:].bitcast(F32), xg[c][:, :, a * P : (a + 1) * P, :], copy)
            if a == 3 and c == 0:
                quantise_x(c)

        def project(c, hf, t0, n, j, vT, sqT):
            acc = psum.tile([P, n], F32, name="acc", tag="bank")
            ch = slice((j % 2) * P, (j % 2 + 1) * P)
            tok = slice(t0, t0 + n)
            for g in range(2):
                nc.tensor.matmul_mx(
                    out=acc[:],
                    lhsT=wq[:, hf, j // 2, g, ch].bitcast(FP8X4),
                    lhsT_scale=wsc[:, hf, j // 2, g, ch],
                    rhs=xq[:, c, g, tok].bitcast(FP8X4),
                    rhs_scale=xsc[:, c, g, tok],
                    start=(g == 0),
                    stop=(g == 1),
                )
            col = slice(8 * hf + j, 8 * hf + j + 1)
            nc.scalar.activation(out=vT[:, j, :], in_=acc[:], func=ACT.Identity, scale=gbT[:, col], bias=gbp[:, col])
            nc.scalar.activation(out=sqT[:, j, :], in_=acc[:], func=ACT.Square, scale=1.0 / ROOT_DM, bias=b32[:, col])

        def finish_unit(c, hf, t0, a, vT, sqT, paired, last=False):
            t = 4 * c + t0 // P + a
            tok = slice(a * P, (a + 1) * P)
            sqacc = psum.tile([P, P], F32, name="sqacc", tag="bank")
            for j in range(NH):
                if j == 1 and paired:
                    continue
                nc.tensor.matmul(
                    out=sqacc[:], lhsT=sqT[:, j, tok], rhs=ident[:], is_transpose=True, start=(j == 0), stop=(j == NH - 1)
                )
            banks = []
            for b in range(2):
                vb = psum.tile([P, BANK], F32, name="vb", tag="bank")
                for jj in range(4):
                    nc.tensor.transpose(vb[:, jj * P : (jj + 1) * P], vT[:, 4 * b + jj, tok], ident[:])
                banks.append(vb)
            junk = small.tile([P, P], BF16, name="junk")
            ms = small.tile([P, 1], F32, name="ms")
            nc.scalar.activation(out=junk[:], in_=sqacc[:], func=ACT.Copy, accum_out=ms[:])
            rstd = small.tile([P, 1], F32, name="rstd")
            nc.scalar.activation(out=rstd[:], in_=ms[:], func=ACT.Abs_reciprocal_sqrt, bias=EPS)
            prod = mmp.tile([P, DM, 2], F32, name="prod")
            for b in range(2):
                nc.vector.scalar_tensor_tensor(
                    out=prod[:, b * BANK : (b + 1) * BANK, :].rearrange("p (h c) t -> p h c t", h=4),
                    in0=banks[b][:].rearrange("p (h c) -> p h c", h=4).unsqueeze(3).to_broadcast([P, 4, P, 2]),
                    scalar=rstd[:, 0:1],
                    in1=rot[:, (t // 4) % 2, t % 4, :].rearrange("p (c t) -> p c t", t=2).unsqueeze(1).to_broadcast([P, 4, P, 2]),
                    op0=ALU.mult,
                    op1=ALU.mult,
                )
            res = outp.tile([P, DM], F32, name="res")
            pairs = prod[:].rearrange("p (j e) t -> p j e t", e=2)
            outpairs = res[:].rearrange("p (j e) -> p j e", e=2)
            if last:
                for b, eng in enumerate((nc.gpsimd, nc.vector)):
                    half = slice(b * BANK, (b + 1) * BANK)
                    hp = slice(b * BANK // 2, (b + 1) * BANK // 2)
                    eng.tensor_tensor(out=outpairs[:, hp, :], in0=pairs[:, hp, :, 0], in1=pairs[:, hp, ::-1, 1], op=ALU.add)
                    nc.sync.dma_start(out=outs[hf][t * P : (t + 1) * P, half], in_=res[:, half])
            else:
                nc.gpsimd.tensor_tensor(out=outpairs, in0=pairs[:, :, :, 0], in1=pairs[:, :, ::-1, 1], op=ALU.add)
                nc.sync.dma_start(out=outs[hf][t * P : (t + 1) * P, :], in_=res[:])

        for pair in range(4):
            prep_x(0, pair)
            prep_w(0, pair)
            load_w(1, pair)
            if pair == 1:
                setup_gain_bias()
                setup_rot()
        load_x(3)
        prep_x(1, 0)
        prep_x(1, 1)

        steps = [(c, hf, 0, FRAME) for c in (0, 1, 2) for hf in (0, 1)]
        steps += [(3, 0, 0, FRAME), (3, 1, 0, 256), (3, 1, 256, 128), (3, 1, 384, 128)]

        prev = None
        for s, (c, hf, t0, n) in enumerate(steps):
            vT = tpose.tile([P, NH, n], F32, name="vT")
            sqT = tpose.tile([P, NH, n], F32, name="sqT")
            units = 0 if prev is None else prev[3] // P
            for part in range(4):
                project(c, hf, t0, n, 2 * part, vT, sqT)
                project(c, hf, t0, n, 2 * part + 1, vT, sqT)
                if part == 0 and n == FRAME:
                    nc.gpsimd.tensor_tensor(out=sqT[:, 0, :], in0=sqT[:, 0, :], in1=sqT[:, 1, :], op=ALU.add)
                if units > 0 and part % (4 // units) == 0:
                    finish_unit(prev[0], prev[1], prev[2], part // (4 // units), prev[4], prev[5], prev[3] == FRAME)
                if s == 0:
                    prep_w(1, part)
                    for i in range((4, 7, 10, 12)[part - 1] if part > 0 else 2, (4, 7, 10, 12)[part]):
                        prep_x(1 + i // 4, i % 4)
                if s in (1, 2, 4) and part == 1:
                    quantise_x(s // 2 + 1)
                if s in (3, 5) and part == 0:
                    spread_frame(s // 2 + 1)
            prev = (c, hf, t0, n, vT, sqT)
        for a in range(prev[3] // P):
            finish_unit(prev[0], prev[1], prev[2], a, prev[4], prev[5], False, last=True)
